import numpy as np
import ml_dtypes


BF16 = ml_dtypes.bfloat16


def bf(x):
    return np.asarray(x, np.float32).astype(BF16)


def f64(x):
    return np.asarray(x).astype(np.float64)


E2M1 = np.array([0.0, 0.5, 1.0, 1.5, 2.0, 3.0, 4.0, 6.0, -0.0, -0.5, -1.0, -1.5, -2.0, -3.0, -4.0, -6.0])


def pack_weight(w, fmt):
    k, n = w.shape
    w = f64(bf(w)).reshape(k // 32, 32, n)
    amax = np.abs(w).max(1)
    if fmt == "e4m3":
        byte = np.frexp(amax)[1] - 1 + 127 - 7
    else:
        mant, ex = np.frexp(amax / 6.0)
        byte = np.where(mant > 0.5, ex, ex - 1) + 127
    byte = np.clip(np.where(amax > 0, byte, 1), 1, 254)
    scaled = (w * np.exp2(127.0 - byte)[:, None, :]).reshape(k, n).astype(np.float32)
    by_word = np.ascontiguousarray(scaled.reshape(k // 512, 128, 4, n).transpose(0, 1, 3, 2))
    if fmt == "e4m3":
        words = by_word.astype(ml_dtypes.float8_e4m3fn).view(np.uint8)
    else:
        c = by_word.astype(ml_dtypes.float4_e2m1fn).view(np.uint8) & 0xF
        words = c[..., 0::2] | (c[..., 1::2] << 4)
    return np.ascontiguousarray(words), np.ascontiguousarray(byte.astype(np.uint8).reshape(k // 512, 16, n))


def unpack_weight(words, scales, fmt):
    g, p, n, _ = words.shape
    if fmt == "e4m3":
        vals = np.ascontiguousarray(words).view(ml_dtypes.float8_e4m3fn).astype(np.float64)
    else:
        nib = np.empty((g, p, n, 4), np.uint8)
        nib[..., 0::2] = words & 0xF
        nib[..., 1::2] = words >> 4
        vals = E2M1[nib]
    vals = vals * np.repeat(np.exp2(scales.astype(np.float64) - 127.0), 8, axis=1)[..., None]
    return vals.transpose(0, 1, 3, 2).reshape(g * 512, n)

def pack4(w):
    words, scales = pack_weight(w, "e2m1")
    return words.reshape(words.shape[0], 128, -1), scales


def unpack4(words, scales):
    return unpack_weight(words.reshape(words.shape[0], 128, -1, 2), scales, "e2m1")


def kspread(k):
    return np.exp2(np.repeat(np.random.randint(-6, 7, k // 32), 32).astype(np.float64))


B, T, D, H, KVH, HD = 2, 512, 4096, 16, 4, 128
HALF = HD // 2
EPS = 1e-6
ROPE_BASE = 10000.0


def zc_rmsnorm(x, scale):
    rms = np.sqrt(np.mean(x ** 2, axis=-1, keepdims=True) + EPS)
    return (1.0 + scale) * x / rms


def apply_rope(x, cos, sin):
    t = x.shape[2]
    c = cos[:t][None, None, :, :]
    s = sin[:t][None, None, :, :]
    x1, x2 = x[..., :HALF], x[..., HALF:]
    return np.concatenate([x1 * c - x2 * s, x2 * c + x1 * s], axis=-1)


def setup_inputs():
    s = kspread(D)
    inv_freq = 1.0 / (ROPE_BASE ** (np.arange(0, HALF) / HALF))
    ang = np.arange(T)[:, None] * inv_freq[None, :]
    kv_input = np.random.standard_normal((B, T, D)) * s
    kv_input_words, kv_input_scales = pack4(np.ascontiguousarray(kv_input.reshape(B * T, D).T))
    Wk_words, Wk_scales = pack4(np.random.standard_normal((D, KVH * HD)) / np.sqrt(D) / s[:, None])
    Wv_words, Wv_scales = pack4(np.random.standard_normal((D, KVH * HD)) / np.sqrt(D) / s[:, None])
    return {"kv_input_words": kv_input_words, "kv_input_scales": kv_input_scales,
            "Wk_words": Wk_words, "Wk_scales": Wk_scales,
            "Wv_words": Wv_words, "Wv_scales": Wv_scales,
            "k_scale": bf(np.random.standard_normal(HD) * 0.2),
            "cos": bf(np.cos(ang)), "sin": bf(np.sin(ang))}


def reference(kv_input_words, kv_input_scales, Wk_words, Wk_scales, Wv_words, Wv_scales, k_scale, cos, sin):
    b = B
    xq = unpack4(kv_input_words, kv_input_scales).T.reshape(B, T, D)
    k = (xq @ unpack4(Wk_words, Wk_scales)).reshape(b, -1, KVH, HD).transpose(0, 2, 1, 3)
    v = (xq @ unpack4(Wv_words, Wv_scales)).reshape(b, -1, KVH, HD).transpose(0, 2, 1, 3)
    k = zc_rmsnorm(k, f64(k_scale))
    rep = H // KVH
    k = np.repeat(k, rep, axis=1)
    v = np.repeat(v, rep, axis=1)
    k = apply_rope(k, f64(cos), f64(sin))
    return k, v

@@ -1,0 +1,197 @@
+from contextlib import ExitStack
+
+import concourse.mybir as mybir
+
+F32 = mybir.dt.float32
+BF16 = mybir.dt.bfloat16
+I32 = mybir.dt.int32
+U8 = mybir.dt.uint8
+FP4X4 = mybir.dt.float4_e2m1fn_x4
+ALU = mybir.AluOpType
+ACT = mybir.ActivationFunctionType
+
+P = 128
+B, T, D, H, KVH, HD = 2, 512, 4096, 16, 4, 128
+HALF = HD // 2
+REP = H // KVH
+C = KVH * HD
+G = D // 512
+TT = T // P
+EPS = 1e-6
+WARM = 8
+
+FLOPS = 2 * B * T * D * 2 * C
+
+
+def tile_multiheadattention_pb_kernel(
+    tc, kv_words, kv_scales, wk_words, wk_scales, wv_words, wv_scales, k_scale, cos, sin, k_out, v_out
+):
+    nc = tc.nc
+    with ExitStack() as ctx:
+        keep = ctx.enter_context(tc.tile_pool(name="keep", bufs=1))
+        outs = ctx.enter_context(tc.tile_pool(name="outs", bufs=8))
+        tmp = ctx.enter_context(tc.tile_pool(name="tmp", bufs=3))
+        psum = ctx.enter_context(tc.psum_pool(name="psum", bufs=7))
+        psum_w = ctx.enter_context(tc.psum_pool(name="psum_w", bufs=1))
+        ctx.enter_context(tc.manual_schedule())
+
+        wv_c = keep.tile([P, G, 2 * C], U8, align_bytes=256)
+        wk_c = keep.tile([P, G, 2 * C], U8, align_bytes=256)
+        kv0_c = keep.tile([P, G, 2 * T], U8, align_bytes=256)
+        kv1_c = keep.tile([P, G, 2 * T], U8, align_bytes=256)
+        wv_s = keep.tile([P, G, C], U8, align_bytes=256)
+        wk_s = keep.tile([P, G, C], U8, align_bytes=256)
+        kv0_s = keep.tile([P, G, T], U8, align_bytes=256)
+        kv1_s = keep.tile([P, G, T], U8, align_bytes=256)
+        kv_c = [kv0_c, kv1_c]
+        kv_s = [kv0_s, kv1_s]
+
+        def as_i32(t):
+            return t[:].rearrange("p g c -> p (g c)").bitcast(I32)
+
+        warm = keep.tile([P, 512], BF16)
+        nc.gpsimd.memset(warm[:], 0.0)
+        nc.vector.memset(as_i32(wv_s), 0)
+        nc.vector.memset(as_i32(kv0_s), 0)
+        nc.gpsimd.memset(as_i32(wk_s), 0)
+        nc.gpsimd.memset(as_i32(kv1_s), 0)
+
+        def load_codes(dst, src, g0, g1):
+            nc.sync.dma_start(
+                out=dst[:, g0:g1, :].bitcast(I32), in_=src[g0:g1].rearrange("g p c -> p g c").bitcast(I32)
+            )
+
+        def load_scales(dst, src):
+            for q in range(4):
+                nc.sync.dma_start(
+                    out=dst[32 * q : 32 * q + 4, :, :].bitcast(I32),
+                    in_=src[:, 4 * q : 4 * q + 4, :].rearrange("g r c -> r g c").bitcast(I32),
+                )
+
+        kvw0 = kv_words[:, :, 0 : 2 * T]
+        kvw1 = kv_words[:, :, 2 * T : 4 * T]
+        load_codes(kv0_c, kvw0, 0, 1)
+        load_codes(wv_c, wv_words, 0, 1)
+        load_scales(wv_s, wv_scales)
+        load_scales(kv0_s, kv_scales[:, :, 0:T])
+        for g0, g1 in ((1, 3), (3, 5), (5, 8)):
+            load_codes(kv0_c, kvw0, g0, g1)
+            load_codes(wv_c, wv_words, g0, g1)
+        load_codes(wk_c, wk_words, 0, 4)
+        load_scales(wk_s, wk_scales)
+        load_codes(wk_c, wk_words, 4, 8)
+        load_codes(kv1_c, kvw1, 0, 4)
+        load_scales(kv1_s, kv_scales[:, :, T : 2 * T])
+        load_codes(kv1_c, kvw1, 4, 8)
+
+        gain_b = keep.tile([P, HD], BF16)
+        nc.gpsimd.dma_start(out=gain_b[:], in_=k_scale.partition_broadcast(P))
+        cos_b = keep.tile([P, TT, HALF], BF16)
+        nc.gpsimd.dma_start(out=cos_b[:], in_=cos.rearrange("(t p) d -> p t d", p=P))
+        sin_b = keep.tile([P, TT, HALF], BF16)
+        nc.gpsimd.dma_start(out=sin_b[:], in_=sin.rearrange("(t p) d -> p t d", p=P))
+
+        zero_c = keep.tile([P, 1], F32)
+        eps_c = keep.tile([P, 1], F32)
+        dummy = keep.tile([P, 1], F32)
+        nc.vector.memset(zero_c[:], 0.0)
+        nc.vector.tensor_scalar(eps_c[:], zero_c[:], 1.0, EPS, op0=ALU.mult, op1=ALU.add)
+        nc.scalar.activation(out=dummy[:], in_=eps_c[:], func=ACT.Abs_reciprocal_sqrt, bias=eps_c[:], scale=1.0 / HD)
+
+        warm_ps = psum_w.tile([P, 512], F32)
+        for w in range(WARM):
+            nc.tensor.matmul(warm_ps[:], lhsT=warm[:, 0:P], rhs=warm[:], start=True, stop=True)
+
+        gain = keep.tile([P, HD], F32)
+        tab_a = keep.tile([P, TT, HD], F32)
+        tab_b = keep.tile([P, TT, HD], F32)
+
+        def tables():
+            nc.vector.tensor_scalar(gain[:], gain_b[:], 1.0, 1.0, op0=ALU.mult, op1=ALU.add)
+            g1 = gain[:, 0:HALF].unsqueeze(1).to_broadcast([P, TT, HALF])
+            g2 = gain[:, HALF:HD].unsqueeze(1).to_broadcast([P, TT, HALF])
+            nc.vector.tensor_tensor(tab_a[:, :, 0:HALF], cos_b[:], g1, op=ALU.mult)
+            nc.vector.tensor_tensor(tab_a[:, :, HALF:HD], cos_b[:], g2, op=ALU.mult)
+            nc.vector.scalar_tensor_tensor(
+                tab_b[:, :, 0:HALF], in0=sin_b[:], scalar=-1.0, in1=g2, op0=ALU.mult, op1=ALU.mult
+            )
+            nc.vector.tensor_tensor(tab_b[:, :, HALF:HD], sin_b[:], g1, op=ALU.mult)
+
+        def mm(acc, b, t, w_c, w_s, g):
+            nc.tensor.matmul_mx(
+                out=acc[:],
+                lhsT=kv_c[b][:, g, 2 * P * t : 2 * P * (t + 1)].bitcast(FP4X4),
+                lhsT_scale=kv_s[b][:, g, P * t : P * (t + 1)],
+                rhs=w_c[:, g, :].bitcast(FP4X4),
+                rhs_scale=w_s[:, g, :],
+                start=(g == 0),
+                stop=(g == G - 1),
+            )
+
+        def store(dst, b, t, src):
+            view = dst[b].rearrange("(j r) n d -> r n j d", r=REP)
+            for r in range(REP):
+                nc.sync.dma_start(
+                    out=view[r, P * t : P * (t + 1)], in_=src[:].rearrange("p (j d) -> p j d", j=KVH)
+                )
+
+        def finish_v(acc, b, t):
+            vt = outs.tile([P, C], F32, tag="vt")
+            nc.scalar.copy(out=vt[:], in_=acc[:])
+            store(v_out, b, t, vt)
+
+        def finish_k(acc, b, t):
+            u = acc[:].rearrange("p (j d) -> p j d", j=KVH)
+            junk = tmp.tile([P, HD], BF16)
+            ss = tmp.tile([P, KVH], F32)
+            rs = tmp.tile([P, KVH], F32)
+            un = tmp.tile([P, KVH, HD], F32)
+            t1 = tmp.tile([P, KVH, HD], F32)
+            t2 = tmp.tile([P, KVH, HD], F32)
+            kt = outs.tile([P, C], F32, tag="kt")
+            for j in range(KVH):
+                nc.scalar.activation(out=junk[:], in_=u[:, j, :], func=ACT.Square, accum_out=ss[:, j : j + 1])
+            nc.scalar.activation(
+                out=rs[:], in_=ss[:], func=ACT.Abs_reciprocal_sqrt, bias=eps_c[:], scale=1.0 / HD
+            )
+            for j in range(KVH):
+                nc.scalar.activation(out=un[:, j, :], in_=u[:, j, :], func=ACT.Copy, scale=rs[:, j : j + 1])
+            a = tab_a[:, t, :].unsqueeze(1).to_broadcast([P, KVH, HD])
+            nc.vector.tensor_tensor(t1[:], un[:], a, op=ALU.mult)
+            b1 = tab_b[:, t, 0:HALF].unsqueeze(1).to_broadcast([P, KVH, HALF])
+            b2 = tab_b[:, t, HALF:HD].unsqueeze(1).to_broadcast([P, KVH, HALF])
+            nc.vector.tensor_tensor(t2[:, :, 0:HALF], un[:, :, HALF:HD], b1, op=ALU.mult)
+            nc.vector.tensor_tensor(t2[:, :, HALF:HD], un[:, :, 0:HALF], b2, op=ALU.mult)
+            nc.vector.tensor_tensor(kt[:].rearrange("p (j d) -> p j d", j=KVH), t1[:], t2[:], op=ALU.add)
+            store(k_out, b, t, kt)
+
+        tables()
+
+        acc_a = psum.tile([P, C], F32, tag="acc")
+        acc_b = psum.tile([P, C], F32, tag="acc")
+        for g in range(G):
+            mm(acc_a, 0, 0, wv_c, wv_s, g)
+            mm(acc_b, 0, 1, wv_c, wv_s, g)
+        finish_v(acc_a, 0, 0)
+        finish_v(acc_b, 0, 1)
+
+        def v_tile(b, t):
+            acc = psum.tile([P, C], F32, tag="acc")
+            for g in range(G):
+                mm(acc, b, t, wv_c, wv_s, g)
+            finish_v(acc, b, t)
+
+        def k_tile(b, t):
+            acc = psum.tile([P, C], F32, tag="acc")
+            for g in range(G):
+                mm(acc, b, t, wk_c, wk_s, g)
+            finish_k(acc, b, t)
+
+        v_tile(0, 2)
+        v_tile(0, 3)
+        for t in range(TT):
+            k_tile(0, t)
+        for t in range(TT):
+            k_tile(1, t)
+        for t in range(TT):
+            v_tile(1, t)

@@ -31,18 +31,23 @@ def tile_multiheadattention_pb_kernel(
         keep = ctx.enter_context(tc.tile_pool(name="keep", bufs=1))
         outs = ctx.enter_context(tc.tile_pool(name="outs", bufs=8))
         tmp = ctx.enter_context(tc.tile_pool(name="tmp", bufs=3))
-        psum = ctx.enter_context(tc.psum_pool(name="psum", bufs=7))
-        psum_w = ctx.enter_context(tc.psum_pool(name="psum_w", bufs=1))
+        psum = ctx.enter_context(tc.psum_pool(name="psum", bufs=8))
         ctx.enter_context(tc.manual_schedule())
 
         wv_c = keep.tile([P, G, 2 * C], U8, align_bytes=256)
         wk_c = keep.tile([P, G, 2 * C], U8, align_bytes=256)
-        kv0_c = keep.tile([P, G, 2 * T], U8, align_bytes=256)
-        kv1_c = keep.tile([P, G, 2 * T], U8, align_bytes=256)
         wv_s = keep.tile([P, G, C], U8, align_bytes=256)
         wk_s = keep.tile([P, G, C], U8, align_bytes=256)
+        raw0_c = keep.tile([P, G, 2 * T], U8, align_bytes=256)
+        raw1_c = keep.tile([P, G, 2 * T], U8, align_bytes=256)
+        raw0_s = keep.tile([P, G, T], U8, align_bytes=256)
+        raw1_s = keep.tile([P, G, T], U8, align_bytes=256)
+        kv0_c = keep.tile([P, G, 2 * T], U8, align_bytes=256)
+        kv1_c = keep.tile([P, G, 2 * T], U8, align_bytes=256)
         kv0_s = keep.tile([P, G, T], U8, align_bytes=256)
         kv1_s = keep.tile([P, G, T], U8, align_bytes=256)
+        raw_c = [raw0_c, raw1_c]
+        raw_s = [raw0_s, raw1_s]
         kv_c = [kv0_c, kv1_c]
         kv_s = [kv0_s, kv1_s]
 
@@ -52,9 +57,9 @@ def tile_multiheadattention_pb_kernel(
         warm = keep.tile([P, 512], BF16)
         nc.gpsimd.memset(warm[:], 0.0)
         nc.vector.memset(as_i32(wv_s), 0)
-        nc.vector.memset(as_i32(kv0_s), 0)
+        nc.vector.memset(as_i32(raw0_s), 0)
+        nc.gpsimd.memset(as_i32(raw1_s), 0)
         nc.gpsimd.memset(as_i32(wk_s), 0)
-        nc.gpsimd.memset(as_i32(kv1_s), 0)
 
         def load_codes(dst, src, g0, g1):
             nc.sync.dma_start(
@@ -70,26 +75,26 @@ def tile_multiheadattention_pb_kernel(
 
         kvw0 = kv_words[:, :, 0 : 2 * T]
         kvw1 = kv_words[:, :, 2 * T : 4 * T]
-        load_codes(kv0_c, kvw0, 0, 1)
+        load_codes(raw0_c, kvw0, 0, 1)
         load_codes(wv_c, wv_words, 0, 1)
+        load_scales(raw0_s, kv_scales[:, :, 0:T])
         load_scales(wv_s, wv_scales)
-        load_scales(kv0_s, kv_scales[:, :, 0:T])
         for g0, g1 in ((1, 3), (3, 5), (5, 8)):
-            load_codes(kv0_c, kvw0, g0, g1)
+            load_codes(raw0_c, kvw0, g0, g1)
             load_codes(wv_c, wv_words, g0, g1)
+        load_codes(raw1_c, kvw1, 0, 4)
+        load_scales(raw1_s, kv_scales[:, :, T : 2 * T])
+        load_codes(raw1_c, kvw1, 4, 8)
         load_codes(wk_c, wk_words, 0, 4)
         load_scales(wk_s, wk_scales)
         load_codes(wk_c, wk_words, 4, 8)
-        load_codes(kv1_c, kvw1, 0, 4)
-        load_scales(kv1_s, kv_scales[:, :, T : 2 * T])
-        load_codes(kv1_c, kvw1, 4, 8)
 
         gain_b = keep.tile([P, HD], BF16)
         nc.gpsimd.dma_start(out=gain_b[:], in_=k_scale.partition_broadcast(P))
         cos_b = keep.tile([P, TT, HALF], BF16)
-        nc.gpsimd.dma_start(out=cos_b[:], in_=cos.rearrange("(t p) d -> p t d", p=P))
+        nc.gpsimd.dma_start(out=cos_b[:], in_=cos.rearrange("(p t) d -> p t d", t=TT))
         sin_b = keep.tile([P, TT, HALF], BF16)
-        nc.gpsimd.dma_start(out=sin_b[:], in_=sin.rearrange("(t p) d -> p t d", p=P))
+        nc.gpsimd.dma_start(out=sin_b[:], in_=sin.rearrange("(p t) d -> p t d", t=TT))
 
         zero_c = keep.tile([P, 1], F32)
         eps_c = keep.tile([P, 1], F32)
@@ -98,9 +103,63 @@ def tile_multiheadattention_pb_kernel(
         nc.vector.tensor_scalar(eps_c[:], zero_c[:], 1.0, EPS, op0=ALU.mult, op1=ALU.add)
         nc.scalar.activation(out=dummy[:], in_=eps_c[:], func=ACT.Abs_reciprocal_sqrt, bias=eps_c[:], scale=1.0 / HD)
 
-        warm_ps = psum_w.tile([P, 512], F32)
+        warm_ps = psum.tile([P, 512], F32, tag="acc")
         for w in range(WARM):
             nc.tensor.matmul(warm_ps[:], lhsT=warm[:, 0:P], rhs=warm[:], start=True, stop=True)
+
+        def permute_codes(b, g):
+            nc.vector.tensor_copy(
+                out=kv_c[b][:, g, :].rearrange("p (t m e) -> p t m e", t=TT, e=2),
+                in_=raw_c[b][:, g, :].rearrange("p (m t e) -> p t m e", t=TT, e=2),
+            )
+
+        def permute_scales(b, g0, g1):
+            nc.vector.tensor_copy(
+                out=kv_s[b][:, g0:g1, :].rearrange("p g (t m) -> p g t m", t=TT),
+                in_=raw_s[b][:, g0:g1, :].rearrange("p g (m t) -> p g t m", t=TT),
+            )
+
+        def mm(acc, b, t, half, w_c, w_s, g):
+            cols = slice(256 * half, 256 * (half + 1))
+            nc.tensor.matmul_mx(
+                out=acc[:],
+                lhsT=kv_c[b][:, g, 2 * P * t : 2 * P * (t + 1)].bitcast(FP4X4),
+                lhsT_scale=kv_s[b][:, g, P * t : P * (t + 1)],
+                rhs=w_c[:, g, 512 * half : 512 * (half + 1)].bitcast(FP4X4),
+                rhs_scale=w_s[:, g, cols],
+                start=(g == 0),
+                stop=(g == G - 1),
+            )
+
+        def store(dst, b, half, src):
+            for jj in range(2):
+                j = 2 * half + jj
+                nc.sync.dma_start(
+                    out=dst[b, REP * j : REP * (j + 1)].rearrange("r (p t) d -> p r (t d)", t=TT),
+                    in_=src[:, jj, :, :].rearrange("p t d -> p (t d)").unsqueeze(1).to_broadcast([P, REP, TT * HD]),
+                )
+
+        def new_acc():
+            acc = psum.tile([P, 2 * HD], F32, tag="acc")
+            return acc
+
+        def new_out():
+            o = outs.tile([P, 2, TT, HD], F32)
+            return o
+
+        def finish_v(acc, o, t):
+            nc.scalar.copy(out=o[:, :, t, :], in_=acc[:].rearrange("p (j d) -> p j d", j=2))
+
+        def norm_k(acc, un, tt):
+            u = acc[:].rearrange("p (j d) -> p j d", j=2)
+            junk = tmp.tile([P, HD], BF16)
+            ss = tmp.tile([P, 2], F32)
+            rs = tmp.tile([P, 2], F32)
+            for jj in range(2):
+                nc.scalar.activation(out=junk[:], in_=u[:, jj, :], func=ACT.Square, accum_out=ss[:, jj : jj + 1])
+            nc.scalar.activation(out=rs[:], in_=ss[:], func=ACT.Abs_reciprocal_sqrt, bias=eps_c[:], scale=1.0 / HD)
+            for jj in range(2):
+                nc.scalar.activation(out=un[:, tt, jj, :], in_=u[:, jj, :], func=ACT.Copy, scale=rs[:, jj : jj + 1])
 
         gain = keep.tile([P, HD], F32)
         tab_a = keep.tile([P, TT, HD], F32)
@@ -117,81 +176,77 @@ def tile_multiheadattention_pb_kernel(
             )
             nc.vector.tensor_tensor(tab_b[:, :, HALF:HD], sin_b[:], g1, op=ALU.mult)
 
-        def mm(acc, b, t, w_c, w_s, g):
-            nc.tensor.matmul_mx(
-                out=acc[:],
-                lhsT=kv_c[b][:, g, 2 * P * t : 2 * P * (t + 1)].bitcast(FP4X4),
-                lhsT_scale=kv_s[b][:, g, P * t : P * (t + 1)],
-                rhs=w_c[:, g, :].bitcast(FP4X4),
-                rhs_scale=w_s[:, g, :],
-                start=(g == 0),
-                stop=(g == G - 1),
+        def rope_k(un, o, t0):
+            t1 = tmp.tile([P, 2, 2, HD], F32)
+            t2 = tmp.tile([P, 2, 2, HD], F32)
+
+            def table(tab, d0, d1):
+                return tab[:, t0 : t0 + 2, d0:d1].unsqueeze(2).to_broadcast([P, 2, 2, d1 - d0])
+
+            nc.vector.tensor_tensor(t1[:], un[:], table(tab_a, 0, HD), op=ALU.mult)
+            nc.vector.tensor_tensor(t2[:, :, :, 0:HALF], un[:, :, :, HALF:HD], table(tab_b, 0, HALF), op=ALU.mult)
+            nc.vector.tensor_tensor(t2[:, :, :, HALF:HD], un[:, :, :, 0:HALF], table(tab_b, HALF, HD), op=ALU.mult)
+            nc.vector.tensor_tensor(
+                o[:, :, t0 : t0 + 2, :].rearrange("p j t d -> p t j d"), t1[:], t2[:], op=ALU.add
             )
 
-        def store(dst, b, t, src):
-            view = dst[b].rearrange("(j r) n d -> r n j d", r=REP)
-            for r in range(REP):
-                nc.sync.dma_start(
-                    out=view[r, P * t : P * (t + 1)], in_=src[:].rearrange("p (j d) -> p j d", j=KVH)
-                )
+        acc0 = [new_acc() for t in range(TT)]
+        acc1 = [new_acc() for t in range(TT)]
+        s_runs = {0: (0, 2), 2: (2, 5), 4: (5, 8)}
+        for g in range(G):
+            permute_codes(0, g)
+            if g in s_runs:
+                permute_scales(0, *s_runs[g])
+            for t in range(TT):
+                mm(acc0[t], 0, t, 0, wv_c, wv_s, g)
+            for t in range(2):
+                mm(acc1[t], 0, t, 1, wv_c, wv_s, g)
+        out0 = new_out()
+        for t in range(TT):
+            finish_v(acc0[t], out0, t)
+        store(v_out, 0, 0, out0)
+        for t in range(2, TT):
+            for g in range(G):
+                mm(acc1[t], 0, t, 1, wv_c, wv_s, g)
+        out1 = new_out()
+        for t in range(TT):
+            finish_v(acc1[t], out1, t)
+        store(v_out, 0, 1, out1)
 
-        def finish_v(acc, b, t):
-            vt = outs.tile([P, C], F32, tag="vt")
-            nc.scalar.copy(out=vt[:], in_=acc[:])
-            store(v_out, b, t, vt)
-
-        def finish_k(acc, b, t):
-            u = acc[:].rearrange("p (j d) -> p j d", j=KVH)
-            junk = tmp.tile([P, HD], BF16)
-            ss = tmp.tile([P, KVH], F32)
-            rs = tmp.tile([P, KVH], F32)
-            un = tmp.tile([P, KVH, HD], F32)
-            t1 = tmp.tile([P, KVH, HD], F32)
-            t2 = tmp.tile([P, KVH, HD], F32)
-            kt = outs.tile([P, C], F32, tag="kt")
-            for j in range(KVH):
-                nc.scalar.activation(out=junk[:], in_=u[:, j, :], func=ACT.Square, accum_out=ss[:, j : j + 1])
-            nc.scalar.activation(
-                out=rs[:], in_=ss[:], func=ACT.Abs_reciprocal_sqrt, bias=eps_c[:], scale=1.0 / HD
-            )
-            for j in range(KVH):
-                nc.scalar.activation(out=un[:, j, :], in_=u[:, j, :], func=ACT.Copy, scale=rs[:, j : j + 1])
-            a = tab_a[:, t, :].unsqueeze(1).to_broadcast([P, KVH, HD])
-            nc.vector.tensor_tensor(t1[:], un[:], a, op=ALU.mult)
-            b1 = tab_b[:, t, 0:HALF].unsqueeze(1).to_broadcast([P, KVH, HALF])
-            b2 = tab_b[:, t, HALF:HD].unsqueeze(1).to_broadcast([P, KVH, HALF])
-            nc.vector.tensor_tensor(t2[:, :, 0:HALF], un[:, :, HALF:HD], b1, op=ALU.mult)
-            nc.vector.tensor_tensor(t2[:, :, HALF:HD], un[:, :, 0:HALF], b2, op=ALU.mult)
-            nc.vector.tensor_tensor(kt[:].rearrange("p (j d) -> p j d", j=KVH), t1[:], t2[:], op=ALU.add)
-            store(k_out, b, t, kt)
-
+        for g in range(G):
+            permute_codes(1, g)
+            if g == 0:
+                permute_scales(1, 0, 4)
+            if g == 4:
+                permute_scales(1, 4, 8)
         tables()
 
-        acc_a = psum.tile([P, C], F32, tag="acc")
-        acc_b = psum.tile([P, C], F32, tag="acc")
-        for g in range(G):
-            mm(acc_a, 0, 0, wv_c, wv_s, g)
-            mm(acc_b, 0, 1, wv_c, wv_s, g)
-        finish_v(acc_a, 0, 0)
-        finish_v(acc_b, 0, 1)
+        for half in range(2):
+            o = new_out()
+            if half == 0:
+                accs = [new_acc() for t in range(TT)]
+                for g in range(G):
+                    for t in range(TT):
+                        mm(accs[t], 1, t, half, wv_c, wv_s, g)
+                for t in range(TT):
+                    finish_v(accs[t], o, t)
+            else:
+                for t in range(TT):
+                    acc = new_acc()
+                    for g in range(G):
+                        mm(acc, 1, t, half, wv_c, wv_s, g)
+                    finish_v(acc, o, t)
+            store(v_out, 1, half, o)
 
-        def v_tile(b, t):
-            acc = psum.tile([P, C], F32, tag="acc")
-            for g in range(G):
-                mm(acc, b, t, wv_c, wv_s, g)
-            finish_v(acc, b, t)
-
-        def k_tile(b, t):
-            acc = psum.tile([P, C], F32, tag="acc")
-            for g in range(G):
-                mm(acc, b, t, wk_c, wk_s, g)
-            finish_k(acc, b, t)
-
-        v_tile(0, 2)
-        v_tile(0, 3)
-        for t in range(TT):
-            k_tile(0, t)
-        for t in range(TT):
-            k_tile(1, t)
-        for t in range(TT):
-            v_tile(1, t)
+        for b in range(B):
+            for half in range(2):
+                o = new_out()
+                for t0 in (0, 2):
+                    un = tmp.tile([P, 2, 2, HD], F32)
+                    for tt in range(2):
+                        acc = new_acc()
+                        for g in range(G):
+                            mm(acc, b, t0 + tt, half, wk_c, wk_s, g)
+                        norm_k(acc, un, tt)
+                    rope_k(un, o, t0)
+                store(k_out, b, half, o)

@@ -56,10 +56,10 @@ def tile_multiheadattention_pb_kernel(
 
         warm = keep.tile([P, 512], BF16)
         nc.gpsimd.memset(warm[:], 0.0)
-        nc.vector.memset(as_i32(wv_s), 0)
         nc.vector.memset(as_i32(raw0_s), 0)
-        nc.gpsimd.memset(as_i32(raw1_s), 0)
-        nc.gpsimd.memset(as_i32(wk_s), 0)
+        nc.vector.memset(as_i32(wv_s), 0)
+        nc.vector.memset(as_i32(raw1_s), 0)
+        nc.vector.memset(as_i32(wk_s), 0)
 
         def load_codes(dst, src, g0, g1):
             nc.sync.dma_start(
@@ -67,10 +67,10 @@ def tile_multiheadattention_pb_kernel(
             )
 
         def load_scales(dst, src):
-            for q in range(4):
+            for r in range(4):
                 nc.sync.dma_start(
-                    out=dst[32 * q : 32 * q + 4, :, :].bitcast(I32),
-                    in_=src[:, 4 * q : 4 * q + 4, :].rearrange("g r c -> r g c").bitcast(I32),
+                    out=dst[r:P:32, :, :].bitcast(I32),
+                    in_=src[:, r:16:4, :].rearrange("g q c -> q g c").bitcast(I32),
                 )
 
         kvw0 = kv_words[:, :, 0 : 2 * T]
@@ -90,7 +90,10 @@ def tile_multiheadattention_pb_kernel(
         load_codes(wk_c, wk_words, 4, 8)
 
         gain_b = keep.tile([P, HD], BF16)
-        nc.gpsimd.dma_start(out=gain_b[:], in_=k_scale.partition_broadcast(P))
+        ones = keep.tile([P, P], BF16)
+        nc.gpsimd.memset(gain_b[:], 0.0)
+        nc.gpsimd.memset(ones[:], 1.0)
+        nc.gpsimd.dma_start(out=gain_b[0:1, :], in_=k_scale.unsqueeze(0))
         cos_b = keep.tile([P, TT, HALF], BF16)
         nc.gpsimd.dma_start(out=cos_b[:], in_=cos.rearrange("(p t) d -> p t d", t=TT))
         sin_b = keep.tile([P, TT, HALF], BF16)
@@ -166,7 +169,9 @@ def tile_multiheadattention_pb_kernel(
         tab_b = keep.tile([P, TT, HD], F32)
 
         def tables():
-            nc.vector.tensor_scalar(gain[:], gain_b[:], 1.0, 1.0, op0=ALU.mult, op1=ALU.add)
+            gain_ps = psum.tile([P, HD], F32, tag="acc")
+            nc.tensor.matmul(gain_ps[:], lhsT=ones[:], rhs=gain_b[:], start=True, stop=True)
+            nc.vector.tensor_scalar(gain[:], gain_ps[:], 1.0, 1.0, op0=ALU.mult, op1=ALU.add)
             g1 = gain[:, 0:HALF].unsqueeze(1).to_broadcast([P, TT, HALF])
             g2 = gain[:, HALF:HD].unsqueeze(1).to_broadcast([P, TT, HALF])
             nc.vector.tensor_tensor(tab_a[:, :, 0:HALF], cos_b[:], g1, op=ALU.mult)

@@ -78,10 +78,13 @@ def tile_multiheadattention_pb_kernel(
         load_codes(raw0_c, kvw0, 0, 1)
         load_codes(wv_c, wv_words, 0, 1)
         load_scales(raw0_s, kv_scales[:, :, 0:T])
+        load_codes(raw0_c, kvw0, 1, 3)
+        load_codes(wv_c, wv_words, 1, 3)
         load_scales(wv_s, wv_scales)
-        for g0, g1 in ((1, 3), (3, 5), (5, 8)):
-            load_codes(raw0_c, kvw0, g0, g1)
-            load_codes(wv_c, wv_words, g0, g1)
+        load_codes(raw0_c, kvw0, 3, 5)
+        load_codes(wv_c, wv_words, 3, 5)
+        load_codes(raw0_c, kvw0, 5, 8)
+        load_codes(wv_c, wv_words, 5, 8)
         load_codes(raw1_c, kvw1, 0, 4)
         load_scales(raw1_s, kv_scales[:, :, T : 2 * T])
         load_codes(raw1_c, kvw1, 4, 8)
@@ -134,44 +137,47 @@ def tile_multiheadattention_pb_kernel(
                 stop=(g == G - 1),
             )
 
-        def store(dst, b, half, src):
-            for jj in range(2):
-                j = 2 * half + jj
-                nc.sync.dma_start(
-                    out=dst[b, REP * j : REP * (j + 1)].rearrange("r (p t) d -> p r (t d)", t=TT),
-                    in_=src[:, jj, :, :].rearrange("p t d -> p (t d)").unsqueeze(1).to_broadcast([P, REP, TT * HD]),
-                )
+        def store(dst, b, j, o):
+            nc.sync.dma_start(
+                out=dst[b, REP * j : REP * (j + 1)].rearrange("r (p t) d -> p r (t d)", t=TT),
+                in_=o[:].rearrange("p t d -> p (t d)").unsqueeze(1).to_broadcast([P, REP, TT * HD]),
+            )
 
         def new_acc():
             acc = psum.tile([P, 2 * HD], F32, tag="acc")
             return acc
 
         def new_out():
-            o = outs.tile([P, 2, TT, HD], F32)
+            o = outs.tile([P, TT, HD], F32)
             return o
 
-        def finish_v(acc, o, t):
-            nc.scalar.copy(out=o[:, :, t, :], in_=acc[:].rearrange("p (j d) -> p j d", j=2))
+        def finish_v(accs, b, half):
+            for jj in range(2):
+                o = new_out()
+                for t in range(TT):
+                    nc.scalar.copy(out=o[:, t, :], in_=accs[t][:, HD * jj : HD * (jj + 1)])
+                store(v_out, b, 2 * half + jj, o)
 
-        def norm_k(acc, un, tt):
-            u = acc[:].rearrange("p (j d) -> p j d", j=2)
-            junk = tmp.tile([P, HD], BF16)
-            ss = tmp.tile([P, 2], F32)
-            rs = tmp.tile([P, 2], F32)
-            for jj in range(2):
-                nc.scalar.activation(out=junk[:], in_=u[:, jj, :], func=ACT.Square, accum_out=ss[:, jj : jj + 1])
+        def norm_k(accs, un):
+            us = [acc[:].rearrange("p (j d) -> p j d", j=2) for acc in accs]
+            junk = tmp.tile([P, 4, HD], BF16)
+            ss = tmp.tile([P, 4], F32)
+            rs = tmp.tile([P, 4], F32)
+            for tt in range(2):
+                for jj in range(2):
+                    i = 2 * tt + jj
+                    nc.scalar.activation(out=junk[:, i, :], in_=us[tt][:, jj, :], func=ACT.Square, accum_out=ss[:, i : i + 1])
             nc.scalar.activation(out=rs[:], in_=ss[:], func=ACT.Abs_reciprocal_sqrt, bias=eps_c[:], scale=1.0 / HD)
-            for jj in range(2):
-                nc.scalar.activation(out=un[:, tt, jj, :], in_=u[:, jj, :], func=ACT.Copy, scale=rs[:, jj : jj + 1])
+            for tt in range(2):
+                for jj in range(2):
+                    i = 2 * tt + jj
+                    nc.scalar.activation(out=un[:, jj, tt, :], in_=us[tt][:, jj, :], func=ACT.Copy, scale=rs[:, i : i + 1])
 
         gain = keep.tile([P, HD], F32)
         tab_a = keep.tile([P, TT, HD], F32)
         tab_b = keep.tile([P, TT, HD], F32)
 
         def tables():
-            gain_ps = psum.tile([P, HD], F32, tag="acc")
-            nc.tensor.matmul(gain_ps[:], lhsT=ones[:], rhs=gain_b[:], start=True, stop=True)
-            nc.vector.tensor_scalar(gain[:], gain_ps[:], 1.0, 1.0, op0=ALU.mult, op1=ALU.add)
             g1 = gain[:, 0:HALF].unsqueeze(1).to_broadcast([P, TT, HALF])
             g2 = gain[:, HALF:HD].unsqueeze(1).to_broadcast([P, TT, HALF])
             nc.vector.tensor_tensor(tab_a[:, :, 0:HALF], cos_b[:], g1, op=ALU.mult)
@@ -181,19 +187,25 @@ def tile_multiheadattention_pb_kernel(
             )
             nc.vector.tensor_tensor(tab_b[:, :, HALF:HD], sin_b[:], g1, op=ALU.mult)
 
-        def rope_k(un, o, t0):
+        def rope_k(un, pair, t0):
             t1 = tmp.tile([P, 2, 2, HD], F32)
-            t2 = tmp.tile([P, 2, 2, HD], F32)
+            t2 = tmp.tile([P, 2, 2, 2, HALF], F32)
+            lo, hi = slice(0, HALF), slice(HALF, HD)
+            for f, out_half, in_half in ((0, lo, hi), (1, hi, lo)):
+                table = tab_b[:, t0 : t0 + 2, out_half].unsqueeze(1).to_broadcast([P, 2, 2, HALF])
+                nc.vector.tensor_tensor(t2[:, f, :, :, :], un[:, :, :, in_half], table, op=ALU.mult)
+            for jj in range(2):
+                nc.vector.tensor_tensor(t1[:, jj, :, :], un[:, jj, :, :], tab_a[:, t0 : t0 + 2, :], op=ALU.mult)
+            for jj in range(2):
+                nc.vector.tensor_tensor(
+                    pair[jj][:, t0 : t0 + 2, :].rearrange("p t (f d) -> p t f d", f=2),
+                    t1[:, jj, :, :].rearrange("p t (f d) -> p t f d", f=2),
+                    t2[:, :, jj, :, :].rearrange("p f t d -> p t f d"),
+                    op=ALU.add,
+                )
 
-            def table(tab, d0, d1):
-                return tab[:, t0 : t0 + 2, d0:d1].unsqueeze(2).to_broadcast([P, 2, 2, d1 - d0])
-
-            nc.vector.tensor_tensor(t1[:], un[:], table(tab_a, 0, HD), op=ALU.mult)
-            nc.vector.tensor_tensor(t2[:, :, :, 0:HALF], un[:, :, :, HALF:HD], table(tab_b, 0, HALF), op=ALU.mult)
-            nc.vector.tensor_tensor(t2[:, :, :, HALF:HD], un[:, :, :, 0:HALF], table(tab_b, HALF, HD), op=ALU.mult)
-            nc.vector.tensor_tensor(
-                o[:, :, t0 : t0 + 2, :].rearrange("p j t d -> p t j d"), t1[:], t2[:], op=ALU.add
-            )
+        gain_ps = psum.tile([P, HD], F32, tag="acc")
+        nc.tensor.matmul(gain_ps[:], lhsT=ones[:], rhs=gain_b[:], start=True, stop=True)
 
         acc0 = [new_acc() for t in range(TT)]
         acc1 = [new_acc() for t in range(TT)]
@@ -202,23 +214,19 @@ def tile_multiheadattention_pb_kernel(
             permute_codes(0, g)
             if g in s_runs:
                 permute_scales(0, *s_runs[g])
+            if g == 0:
+                nc.vector.tensor_scalar(gain[:], gain_ps[:], 1.0, 1.0, op0=ALU.mult, op1=ALU.add)
             for t in range(TT):
                 mm(acc0[t], 0, t, 0, wv_c, wv_s, g)
             for t in range(2):
                 mm(acc1[t], 0, t, 1, wv_c, wv_s, g)
-        out0 = new_out()
-        for t in range(TT):
-            finish_v(acc0[t], out0, t)
-        store(v_out, 0, 0, out0)
+        finish_v(acc0, 0, 0)
         for t in range(2, TT):
             for g in range(G):
                 mm(acc1[t], 0, t, 1, wv_c, wv_s, g)
-        out1 = new_out()
-        for t in range(TT):
-            finish_v(acc1[t], out1, t)
-        store(v_out, 0, 1, out1)
+        finish_v(acc1, 0, 1)
 
-        for g in range(G):
+        for g in range(8):
             permute_codes(1, g)
             if g == 0:
                 permute_scales(1, 0, 4)
@@ -227,31 +235,27 @@ def tile_multiheadattention_pb_kernel(
         tables()
 
         for half in range(2):
-            o = new_out()
+            accs = [new_acc() for t in range(TT)]
             if half == 0:
-                accs = [new_acc() for t in range(TT)]
                 for g in range(G):
                     for t in range(TT):
                         mm(accs[t], 1, t, half, wv_c, wv_s, g)
-                for t in range(TT):
-                    finish_v(accs[t], o, t)
             else:
                 for t in range(TT):
-                    acc = new_acc()
                     for g in range(G):
-                        mm(acc, 1, t, half, wv_c, wv_s, g)
-                    finish_v(acc, o, t)
-            store(v_out, 1, half, o)
+                        mm(accs[t], 1, t, half, wv_c, wv_s, g)
+            finish_v(accs, 1, half)
 
         for b in range(B):
             for half in range(2):
-                o = new_out()
+                pair = [new_out() for jj in range(2)]
                 for t0 in (0, 2):
                     un = tmp.tile([P, 2, 2, HD], F32)
+                    accs = [new_acc() for tt in range(2)]
                     for tt in range(2):
-                        acc = new_acc()
                         for g in range(G):
-                            mm(acc, b, t0 + tt, half, wk_c, wk_s, g)
-                        norm_k(acc, un, tt)
-                    rope_k(un, o, t0)
-                store(k_out, b, half, o)
+                            mm(accs[tt], b, t0 + tt, half, wk_c, wk_s, g)
+                    norm_k(accs, un)
+                    rope_k(un, pair, t0)
+                for jj in range(2):
+                    store(k_out, b, 2 * half + jj, pair[jj])

from contextlib import ExitStack

import concourse.mybir as mybir

F32 = mybir.dt.float32
BF16 = mybir.dt.bfloat16
I32 = mybir.dt.int32
U8 = mybir.dt.uint8
FP4X4 = mybir.dt.float4_e2m1fn_x4
ALU = mybir.AluOpType
ACT = mybir.ActivationFunctionType

P = 128
B, T, D, H, KVH, HD = 2, 512, 4096, 16, 4, 128
HALF = HD // 2
REP = H // KVH
C = KVH * HD
G = D // 512
TT = T // P
EPS = 1e-6
WARM = 8

FLOPS = 2 * B * T * D * 2 * C


def tile_multiheadattention_pb_kernel(
    tc, kv_words, kv_scales, wk_words, wk_scales, wv_words, wv_scales, k_scale, cos, sin, k_out, v_out
):
    nc = tc.nc
    with ExitStack() as ctx:
        keep = ctx.enter_context(tc.tile_pool(name="keep", bufs=1))
        outs = ctx.enter_context(tc.tile_pool(name="outs", bufs=8))
        tmp = ctx.enter_context(tc.tile_pool(name="tmp", bufs=3))
        psum = ctx.enter_context(tc.psum_pool(name="psum", bufs=8))
        ctx.enter_context(tc.manual_schedule())

        wv_c = keep.tile([P, G, 2 * C], U8, align_bytes=256)
        wk_c = keep.tile([P, G, 2 * C], U8, align_bytes=256)
        wv_s = keep.tile([P, G, C], U8, align_bytes=256)
        wk_s = keep.tile([P, G, C], U8, align_bytes=256)
        raw0_c = keep.tile([P, G, 2 * T], U8, align_bytes=256)
        raw1_c = keep.tile([P, G, 2 * T], U8, align_bytes=256)
        raw0_s = keep.tile([P, G, T], U8, align_bytes=256)
        raw1_s = keep.tile([P, G, T], U8, align_bytes=256)
        kv0_c = keep.tile([P, G, 2 * T], U8, align_bytes=256)
        kv1_c = keep.tile([P, G, 2 * T], U8, align_bytes=256)
        kv0_s = keep.tile([P, G, T], U8, align_bytes=256)
        kv1_s = keep.tile([P, G, T], U8, align_bytes=256)
        raw_c = [raw0_c, raw1_c]
        raw_s = [raw0_s, raw1_s]
        kv_c = [kv0_c, kv1_c]
        kv_s = [kv0_s, kv1_s]

        def as_i32(t):
            return t[:].rearrange("p g c -> p (g c)").bitcast(I32)

        warm = keep.tile([P, 512], BF16)
        nc.gpsimd.memset(warm[:], 0.0)
        nc.vector.memset(as_i32(raw0_s), 0)
        nc.vector.memset(as_i32(wv_s), 0)
        nc.vector.memset(as_i32(raw1_s), 0)
        nc.vector.memset(as_i32(wk_s), 0)

        def load_codes(dst, src, g0, g1):
            nc.sync.dma_start(
                out=dst[:, g0:g1, :].bitcast(I32), in_=src[g0:g1].rearrange("g p c -> p g c").bitcast(I32)
            )

        def load_scales(dst, src):
            for r in range(4):
                nc.sync.dma_start(
                    out=dst[r:P:32, :, :].bitcast(I32),
                    in_=src[:, r:16:4, :].rearrange("g q c -> q g c").bitcast(I32),
                )

        kvw0 = kv_words[:, :, 0 : 2 * T]
        kvw1 = kv_words[:, :, 2 * T : 4 * T]
        load_codes(raw0_c, kvw0, 0, 1)
        load_codes(wv_c, wv_words, 0, 1)
        load_scales(raw0_s, kv_scales[:, :, 0:T])
        load_codes(raw0_c, kvw0, 1, 3)
        load_codes(wv_c, wv_words, 1, 3)
        load_scales(wv_s, wv_scales)
        load_codes(raw0_c, kvw0, 3, 5)
        load_codes(wv_c, wv_words, 3, 5)
        load_codes(raw0_c, kvw0, 5, 8)
        load_codes(wv_c, wv_words, 5, 8)
        load_codes(raw1_c, kvw1, 0, 4)
        load_scales(raw1_s, kv_scales[:, :, T : 2 * T])
        load_codes(raw1_c, kvw1, 4, 8)
        load_codes(wk_c, wk_words, 0, 4)
        load_scales(wk_s, wk_scales)
        load_codes(wk_c, wk_words, 4, 8)

        gain_b = keep.tile([P, HD], BF16)
        ones = keep.tile([P, P], BF16)
        nc.gpsimd.memset(gain_b[:], 0.0)
        nc.gpsimd.memset(ones[:], 1.0)
        nc.gpsimd.dma_start(out=gain_b[0:1, :], in_=k_scale.unsqueeze(0))
        cos_b = keep.tile([P, TT, HALF], BF16)
        nc.gpsimd.dma_start(out=cos_b[:], in_=cos.rearrange("(p t) d -> p t d", t=TT))
        sin_b = keep.tile([P, TT, HALF], BF16)
        nc.gpsimd.dma_start(out=sin_b[:], in_=sin.rearrange("(p t) d -> p t d", t=TT))

        zero_c = keep.tile([P, 1], F32)
        eps_c = keep.tile([P, 1], F32)
        dummy = keep.tile([P, 1], F32)
        nc.vector.memset(zero_c[:], 0.0)
        nc.vector.tensor_scalar(eps_c[:], zero_c[:], 1.0, EPS, op0=ALU.mult, op1=ALU.add)
        nc.scalar.activation(out=dummy[:], in_=eps_c[:], func=ACT.Abs_reciprocal_sqrt, bias=eps_c[:], scale=1.0 / HD)

        warm_ps = psum.tile([P, 512], F32, tag="acc")
        for w in range(WARM):
            nc.tensor.matmul(warm_ps[:], lhsT=warm[:, 0:P], rhs=warm[:], start=True, stop=True)

        def permute_codes(b, g):
            nc.vector.tensor_copy(
                out=kv_c[b][:, g, :].rearrange("p (t m e) -> p t m e", t=TT, e=2),
                in_=raw_c[b][:, g, :].rearrange("p (m t e) -> p t m e", t=TT, e=2),
            )

        def permute_scales(b, g0, g1):
            nc.vector.tensor_copy(
                out=kv_s[b][:, g0:g1, :].rearrange("p g (t m) -> p g t m", t=TT),
                in_=raw_s[b][:, g0:g1, :].rearrange("p g (m t) -> p g t m", t=TT),
            )

        def mm(acc, b, t, half, w_c, w_s, g):
            cols = slice(256 * half, 256 * (half + 1))
            nc.tensor.matmul_mx(
                out=acc[:],
                lhsT=kv_c[b][:, g, 2 * P * t : 2 * P * (t + 1)].bitcast(FP4X4),
                lhsT_scale=kv_s[b][:, g, P * t : P * (t + 1)],
                rhs=w_c[:, g, 512 * half : 512 * (half + 1)].bitcast(FP4X4),
                rhs_scale=w_s[:, g, cols],
                start=(g == 0),
                stop=(g == G - 1),
            )

        def store(dst, b, j, o):
            nc.sync.dma_start(
                out=dst[b, REP * j : REP * (j + 1)].rearrange("r (p t) d -> p r (t d)", t=TT),
                in_=o[:].rearrange("p t d -> p (t d)").unsqueeze(1).to_broadcast([P, REP, TT * HD]),
            )

        def new_acc():
            acc = psum.tile([P, 2 * HD], F32, tag="acc")
            return acc

        def new_out():
            o = outs.tile([P, TT, HD], F32)
            return o

        def finish_v(accs, b, half):
            for jj in range(2):
                o = new_out()
                for t in range(TT):
                    nc.scalar.copy(out=o[:, t, :], in_=accs[t][:, HD * jj : HD * (jj + 1)])
                store(v_out, b, 2 * half + jj, o)

        def norm_k(accs, un):
            us = [acc[:].rearrange("p (j d) -> p j d", j=2) for acc in accs]
            junk = tmp.tile([P, 4, HD], BF16)
            ss = tmp.tile([P, 4], F32)
            rs = tmp.tile([P, 4], F32)
            for tt in range(2):
                for jj in range(2):
                    i = 2 * tt + jj
                    nc.scalar.activation(out=junk[:, i, :], in_=us[tt][:, jj, :], func=ACT.Square, accum_out=ss[:, i : i + 1])
            nc.scalar.activation(out=rs[:], in_=ss[:], func=ACT.Abs_reciprocal_sqrt, bias=eps_c[:], scale=1.0 / HD)
            for tt in range(2):
                for jj in range(2):
                    i = 2 * tt + jj
                    nc.scalar.activation(out=un[:, jj, tt, :], in_=us[tt][:, jj, :], func=ACT.Copy, scale=rs[:, i : i + 1])

        gain = keep.tile([P, HD], F32)
        tab_a = keep.tile([P, TT, HD], F32)
        tab_b = keep.tile([P, TT, HD], F32)

        def tables():
            g1 = gain[:, 0:HALF].unsqueeze(1).to_broadcast([P, TT, HALF])
            g2 = gain[:, HALF:HD].unsqueeze(1).to_broadcast([P, TT, HALF])
            nc.vector.tensor_tensor(tab_a[:, :, 0:HALF], cos_b[:], g1, op=ALU.mult)
            nc.vector.tensor_tensor(tab_a[:, :, HALF:HD], cos_b[:], g2, op=ALU.mult)
            nc.vector.scalar_tensor_tensor(
                tab_b[:, :, 0:HALF], in0=sin_b[:], scalar=-1.0, in1=g2, op0=ALU.mult, op1=ALU.mult
            )
            nc.vector.tensor_tensor(tab_b[:, :, HALF:HD], sin_b[:], g1, op=ALU.mult)

        def rope_k(un, pair, t0):
            t1 = tmp.tile([P, 2, 2, HD], F32)
            t2 = tmp.tile([P, 2, 2, 2, HALF], F32)
            lo, hi = slice(0, HALF), slice(HALF, HD)
            for f, out_half, in_half in ((0, lo, hi), (1, hi, lo)):
                table = tab_b[:, t0 : t0 + 2, out_half].unsqueeze(1).to_broadcast([P, 2, 2, HALF])
                nc.vector.tensor_tensor(t2[:, f, :, :, :], un[:, :, :, in_half], table, op=ALU.mult)
            for jj in range(2):
                nc.vector.tensor_tensor(t1[:, jj, :, :], un[:, jj, :, :], tab_a[:, t0 : t0 + 2, :], op=ALU.mult)
            for jj in range(2):
                nc.vector.tensor_tensor(
                    pair[jj][:, t0 : t0 + 2, :].rearrange("p t (f d) -> p t f d", f=2),
                    t1[:, jj, :, :].rearrange("p t (f d) -> p t f d", f=2),
                    t2[:, :, jj, :, :].rearrange("p f t d -> p t f d"),
                    op=ALU.add,
                )

        gain_ps = psum.tile([P, HD], F32, tag="acc")
        nc.tensor.matmul(gain_ps[:], lhsT=ones[:], rhs=gain_b[:], start=True, stop=True)

        acc0 = [new_acc() for t in range(TT)]
        acc1 = [new_acc() for t in range(TT)]
        s_runs = {0: (0, 2), 2: (2, 5), 4: (5, 8)}
        for g in range(G):
            permute_codes(0, g)
            if g in s_runs:
                permute_scales(0, *s_runs[g])
            if g == 0:
                nc.vector.tensor_scalar(gain[:], gain_ps[:], 1.0, 1.0, op0=ALU.mult, op1=ALU.add)
            for t in range(TT):
                mm(acc0[t], 0, t, 0, wv_c, wv_s, g)
            for t in range(2):
                mm(acc1[t], 0, t, 1, wv_c, wv_s, g)
        finish_v(acc0, 0, 0)
        for t in range(2, TT):
            for g in range(G):
                mm(acc1[t], 0, t, 1, wv_c, wv_s, g)
        finish_v(acc1, 0, 1)

        for g in range(8):
            permute_codes(1, g)
            if g == 0:
                permute_scales(1, 0, 4)
            if g == 4:
                permute_scales(1, 4, 8)
        tables()

        for half in range(2):
            accs = [new_acc() for t in range(TT)]
            if half == 0:
                for g in range(G):
                    for t in range(TT):
                        mm(accs[t], 1, t, half, wv_c, wv_s, g)
            else:
                for t in range(TT):
                    for g in range(G):
                        mm(accs[t], 1, t, half, wv_c, wv_s, g)
            finish_v(accs, 1, half)

        for b in range(B):
            for half in range(2):
                pair = [new_out() for jj in range(2)]
                for t0 in (0, 2):
                    un = tmp.tile([P, 2, 2, HD], F32)
                    accs = [new_acc() for tt in range(2)]
                    for tt in range(2):
                        for g in range(G):
                            mm(accs[tt], b, t0 + tt, half, wk_c, wk_s, g)
                    norm_k(accs, un)
                    rope_k(un, pair, t0)
                for jj in range(2):
                    store(k_out, b, 2 * half + jj, pair[jj])
